import numpy as np
import ml_dtypes


def mxq(x, axis, fmt="e4m3"):
    dtype, down = {"e4m3": (ml_dtypes.float8_e4m3fn, 7), "e5m2": (ml_dtypes.float8_e5m2, 14)}[fmt]
    v = np.moveaxis(np.asarray(x, np.float32).astype(ml_dtypes.bfloat16).astype(np.float64), axis, -1)
    blocks = v.reshape(v.shape[:-1] + (-1, 32))
    amax = np.abs(blocks).max(-1, keepdims=True)
    byte = np.maximum(np.where(amax > 0, np.frexp(amax)[1] - 1 + 127, 0) - down, 1)
    scale = np.exp2(byte - 127.0)
    codes = (blocks / scale).astype(np.float32).astype(dtype).astype(np.float64)
    return np.moveaxis((codes * scale).reshape(v.shape), -1, axis)


WIDE = False


def mx_kscale(k):
    if not WIDE:
        return np.ones(k)
    levels = np.array([10, -10, 5, -5, 0])
    if k % 512:
        return np.exp2(np.random.permutation(np.resize(levels, k // 32))).repeat(32)
    a = np.empty((k // 512, 16))
    for p in range(k // 512):
        a[p, :8] = np.random.permutation(np.resize(levels, 8))
        for g in range(8):
            far = levels[np.abs(levels - a[p, g]) >= 10]
            a[p, g + 8] = far[np.random.randint(len(far))]
    return np.exp2(a.ravel()).repeat(32)


BF16 = ml_dtypes.bfloat16


def bf(x):
    return np.asarray(x, np.float32).astype(BF16)


def f64(x):
    return np.asarray(x).astype(np.float64)


B, N, R, DE, DR, NUM_BASES, OUT_DIM = 1, 1024, 16, 128, 64, 256, 128
F = DE + DR
KS = R * F


def setup_inputs():
    s = mx_kscale(N)
    t = mx_kscale(KS)[:F]
    deg = np.random.uniform(0.5, 1.5, (B, R, N, 1))
    adj = np.random.uniform(0.0, 1.0, (B, R, N, N)) * deg / np.sqrt(N)
    return {"node_features": bf(np.random.standard_normal((B, N, DE)) * 2.0 / s[:, None] * t[:DE]),
            "relation_features": bf(np.random.standard_normal((B, R, DR)) * 2.0 / np.sqrt(N) / s.mean() * t[DE:]),
            "adj": bf(adj * s),
            "Wb": bf(np.random.standard_normal((NUM_BASES, KS)) / np.sqrt(KS) / np.tile(t, R))}


def reference(node_features, relation_features, adj, Wb):
    a = f64(adj)
    node_part = mxq(a, 3, "e4m3") @ mxq(f64(node_features), 1, "e4m3")[:, None]
    row_sum = a.sum(-1)
    rel_part = row_sum[..., None] * f64(relation_features)[:, :, None, :]
    supports = np.concatenate([node_part, rel_part], -1)
    supports = supports.transpose(0, 2, 1, 3).reshape(B, N, KS)
    return mxq(supports, 2, "e4m3") @ mxq(f64(Wb), 1, "e4m3").T

@@ -1,0 +1,385 @@
+from contextlib import ExitStack
+
+import concourse.masks as masks
+import concourse.mybir as mybir
+
+F32 = mybir.dt.float32
+BF16 = mybir.dt.bfloat16
+U32 = mybir.dt.uint32
+U8 = mybir.dt.uint8
+FP8X4 = mybir.dt.float8_e4m3fn_x4
+ALU = mybir.AluOpType
+AXIS = mybir.AxisListType
+
+P = 128
+PACK = 4
+K_PASS = P * PACK
+
+NODES = 1024
+RELATIONS = 16
+D_NODE = 128
+D_REL = 64
+D_SUPPORT = D_NODE + D_REL
+BASES = 256
+BASE_HALVES = BASES // P
+
+GROUP = 4
+N_GROUPS = RELATIONS // GROUP
+N_BLOCKS = NODES // P
+N_ROUNDS = N_BLOCKS * N_GROUPS
+J_PASSES = NODES // K_PASS
+KS = RELATIONS * D_SUPPORT
+SUP_PASSES = KS // K_PASS
+
+TENSOR_SUMS = 2
+VECTOR_SUMS = GROUP - TENSOR_SUMS
+BLOCK_TENSOR_SUMS = N_GROUPS * TENSOR_SUMS
+ROWS_PER_SUM = P // PACK
+SUMS_PER_BLOCK = P // ROWS_PER_SUM
+SUM_WIDTH = 32
+
+QUANTISE_LAG = 1
+MULTIPLY_LAG = 2
+COLLECT_LAG = 1
+GATHER_LAG = 2
+TURN_LAG = 3
+SUPPORT_LAG = 4
+PROJECT_LAG = 5
+WEIGHT_STEP = 2
+
+FLOPS = 2 * RELATIONS * NODES * NODES * D_NODE + 2 * NODES * RELATIONS * D_SUPPORT * BASES
+
+
+def is_round(n):
+    return 0 <= n < N_ROUNDS
+
+
+def block_ending_with(n):
+    if is_round(n) and n % N_GROUPS == N_GROUPS - 1:
+        return n // N_GROUPS
+    return None
+
+
+def tile_relationalgraphconvolution_pa_kernel(
+    tc, node_features, relation_features, adj, Wb, out
+):
+    nc = tc.nc
+    with ExitStack() as ctx:
+        ctx.enter_context(tc.manual_schedule())
+        const = ctx.enter_context(tc.tile_pool(name="const", bufs=1))
+        adj_pool = ctx.enter_context(tc.tile_pool(name="adj", bufs=4))
+        round_pool = ctx.enter_context(tc.tile_pool(name="round", bufs=3))
+        block_pool = ctx.enter_context(tc.tile_pool(name="block", bufs=2))
+        turned_psum = ctx.enter_context(tc.psum_pool(name="turned", bufs=4))
+        node_psum = ctx.enter_context(tc.psum_pool(name="node", bufs=2))
+        single_psum = ctx.enter_context(tc.psum_pool(name="single", bufs=1))
+
+        ident_f32 = const.tile([P, P], F32)
+        masks.make_identity(nc, ident_f32[:])
+        ones = const.tile([P, SUM_WIDTH], BF16)
+        nc.vector.memset(ones[:], 1.0)
+        gather = const.tile([P, SUMS_PER_BLOCK, P], F32)
+        nc.vector.memset(gather[:], 0.0)
+        for s in range(SUMS_PER_BLOCK):
+            nc.vector.tensor_reduce(
+                out=gather[:, s, s * ROWS_PER_SUM : (s + 1) * ROWS_PER_SUM],
+                in_=ident_f32[:].rearrange("k (x t) -> k x t", t=PACK),
+                axis=AXIS.X,
+                op=ALU.add,
+            )
+
+        nf_rows = const.tile([P, J_PASSES, PACK * D_NODE], BF16)
+        nc.sync.dma_start(
+            out=nf_rows[:],
+            in_=node_features[0].rearrange("(c p t) d -> p c (t d)", p=P, t=PACK),
+        )
+        nf_grouped = const.tile([P, J_PASSES, D_NODE, PACK], BF16, align_bytes=64)
+        for c in range(J_PASSES):
+            for u in range(2):
+                nc.vector.tensor_copy(
+                    out=nf_grouped[:, c, u * D_NODE // 2 : (u + 1) * D_NODE // 2, :].rearrange(
+                        "p (x e) t -> p x e t", e=2
+                    ),
+                    in_=nf_rows[:, c, :].rearrange("p (t x u e) -> p u x e t", t=PACK, u=2, e=2)[
+                        :, u
+                    ],
+                )
+        nf_codes = const.tile([P, J_PASSES * D_NODE], U32, align_bytes=64)
+        nf_scales = const.tile([P, J_PASSES * D_NODE], U8, align_bytes=64)
+        nc.vector.quantize_mx(
+            out=nf_codes[:].bitcast(FP8X4),
+            scales=nf_scales[:],
+            in_=nf_grouped[:].rearrange("p c d t -> p (c d t)"),
+        )
+
+        w_codes = const.tile([P, SUP_PASSES * BASES], U32, align_bytes=64)
+        w_scales = const.tile([P, SUP_PASSES * BASES], U8, align_bytes=64)
+        relf_turned = const.tile([P, 2, RELATIONS, D_REL // 2], BF16)
+
+        def prepare_weights():
+            w_rows = const.tile([P, BASE_HALVES, KS], BF16)
+            nc.sync.dma_start(out=w_rows[:], in_=Wb.rearrange("(h p) k -> p h k", p=P))
+            relf_all = const.tile([P, RELATIONS * D_REL], BF16)
+            nc.sync.dma_start(
+                out=relf_all[:],
+                in_=relation_features[0].rearrange("r e -> (r e)").partition_broadcast(P),
+            )
+            nc.vector.tensor_copy(
+                out=relf_turned[:].rearrange("p u r (x e) -> p u (r x) e", e=2),
+                in_=relf_all[:].rearrange("p (rx u e) -> p u rx e", u=2, e=2),
+            )
+            w_words = w_rows[:].rearrange("p h k -> p (h k)").bitcast(F32)
+            w_grouped = const.tile([P, SUP_PASSES, BASES * PACK], BF16, align_bytes=64)
+            for q in range(SUP_PASSES):
+                w_t = turned_psum.tile([P, BASE_HALVES, 2, P], F32, tag="turned")
+                for h in range(BASE_HALVES):
+                    for u in range(2):
+                        first = h * (KS // 2) + q * 2 * P + u
+                        nc.tensor.transpose(
+                            out=w_t[:, h, u, :],
+                            in_=w_words[:, first : first + 2 * P - 1 : 2],
+                            identity=ident_f32[:],
+                        )
+                copy = nc.vector.tensor_copy if q % 2 == 0 else nc.scalar.copy
+                copy(
+                    out=w_grouped[:, q].bitcast(F32).rearrange("p (h b u) -> p h b u", h=BASE_HALVES, u=2),
+                    in_=w_t[:].rearrange("p h u b -> p h b u"),
+                )
+            w_flat = w_grouped[:].rearrange("p q x -> p (q x)")
+            for first, width in ((0, 4 * BASES), (4 * BASES, 2 * BASES)):
+                nc.vector.quantize_mx(
+                    out=w_codes[:, first : first + width].bitcast(FP8X4),
+                    scales=w_scales[:, first : first + width],
+                    in_=w_flat[:, PACK * first : PACK * (first + width)],
+                )
+
+        a_rows = {}
+        grouped = {}
+        a_codes = {}
+        a_scales = {}
+        sums_vector = {}
+        sums_psum = {}
+        sup_rows = {}
+        sup_grouped = {}
+
+        def load_round(n):
+            block, group = divmod(n, N_GROUPS)
+            a_tile = adj_pool.tile([P, GROUP * NODES], BF16)
+            nc.sync.dma_start(
+                out=a_tile[:].rearrange("i (r j) -> i r j", r=GROUP),
+                in_=adj[
+                    0, group * GROUP : (group + 1) * GROUP, block * P : (block + 1) * P, :
+                ].rearrange("r i j -> i r j"),
+            )
+            a_rows[n] = a_tile
+
+        def sum_on_vector(n):
+            block, group = divmod(n, N_GROUPS)
+            if group == 0:
+                sums_tile = block_pool.tile([P, N_GROUPS, VECTOR_SUMS], F32)
+                sums_vector[block] = sums_tile
+            for v in range(VECTOR_SUMS):
+                r = TENSOR_SUMS + v
+                scratch = round_pool.tile([P, NODES], BF16)
+                nc.vector.tensor_scalar(
+                    out=scratch[:],
+                    in0=a_rows[n][:, r * NODES : (r + 1) * NODES],
+                    scalar1=1.0,
+                    scalar2=None,
+                    op0=ALU.mult,
+                    op1=ALU.add,
+                    accum_out=sums_vector[block][:, group, v : v + 1],
+                )
+
+        def transpose_round(n):
+            a_words = a_rows[n][:].bitcast(F32)
+            g_tile = round_pool.tile([P, GROUP * NODES], BF16, align_bytes=64)
+            g_words = g_tile[:].bitcast(F32).rearrange(
+                "p (r c i u) -> p r c i u", r=GROUP, c=J_PASSES, u=2
+            )
+            for r in range(GROUP):
+                a_t = turned_psum.tile([P, PACK, P], F32, tag="turned")
+                for c in range(J_PASSES):
+                    for u in range(2):
+                        first = r * (NODES // 2) + c * 2 * P + u
+                        nc.tensor.transpose(
+                            out=a_t[:, 2 * c + u, :],
+                            in_=a_words[:, first : first + 2 * P - 1 : 2],
+                            identity=ident_f32[:],
+                        )
+                nc.scalar.copy(
+                    out=g_words[:, r], in_=a_t[:].rearrange("p (c u) i -> p c i u", u=2)
+                )
+            grouped[n] = g_tile
+
+        def sum_on_tensor(n):
+            block, group = divmod(n, N_GROUPS)
+            if group == 0:
+                sums_tile = single_psum.tile(
+                    [P, BLOCK_TENSOR_SUMS * SUMS_PER_BLOCK + SUM_WIDTH - 1], F32
+                )
+                sums_psum[block] = sums_tile
+            for r in range(TENSOR_SUMS):
+                for s in range(SUMS_PER_BLOCK):
+                    column = (group * TENSOR_SUMS + r) * SUMS_PER_BLOCK + s
+                    for c in range(J_PASSES):
+                        first = ((r * J_PASSES + c) * P + s * ROWS_PER_SUM) * PACK
+                        nc.tensor.matmul(
+                            out=sums_psum[block][:, column : column + SUM_WIDTH],
+                            lhsT=grouped[n][:, first : first + P],
+                            rhs=ones[:],
+                            start=(c == 0),
+                            stop=(c == J_PASSES - 1),
+                        )
+
+        def quantise_round(n):
+            codes = round_pool.tile([P, GROUP * J_PASSES * P], U32, align_bytes=64)
+            scales = round_pool.tile([P, GROUP * J_PASSES * P], U8, align_bytes=64)
+            nc.vector.quantize_mx(out=codes[:].bitcast(FP8X4), scales=scales[:], in_=grouped[n][:])
+            a_codes[n] = codes
+            a_scales[n] = scales
+
+        def multiply_round(n):
+            block, group = divmod(n, N_GROUPS)
+            if group == 0:
+                rows_tile = block_pool.tile([P, 2, RELATIONS, D_SUPPORT // 2], BF16)
+                sup_rows[block] = rows_tile
+            node = node_psum.tile([P, GROUP, D_NODE], F32, tag="node")
+            for r in range(GROUP):
+                for c in range(J_PASSES):
+                    a_cols = slice((r * J_PASSES + c) * P, (r * J_PASSES + c + 1) * P)
+                    nf_cols = slice(c * D_NODE, (c + 1) * D_NODE)
+                    nc.tensor.matmul_mx(
+                        out=node[:, r, :],
+                        lhsT=a_codes[n][:, a_cols].bitcast(FP8X4),
+                        lhsT_scale=a_scales[n][:, a_cols],
+                        rhs=nf_codes[:, nf_cols].bitcast(FP8X4),
+                        rhs_scale=nf_scales[:, nf_cols],
+                        start=(c == 0),
+                        stop=(c == J_PASSES - 1),
+                    )
+            nc.scalar.copy(
+                out=sup_rows[block][:].rearrange("i u r x -> i r u x")[
+                    :, group * GROUP : (group + 1) * GROUP, :, 0 : D_NODE // 2
+                ],
+                in_=node[:].rearrange("i r (u x) -> i r u x", u=2),
+            )
+
+        partial = {}
+        sums_tensor = {}
+        sup_codes = {}
+        sup_scales = {}
+
+        def collect_sums(block):
+            partial_tile = block_pool.tile([P, SUMS_PER_BLOCK * BLOCK_TENSOR_SUMS], F32)
+            nc.scalar.copy(
+                out=partial_tile[:].rearrange("k (s x) -> k s x", s=SUMS_PER_BLOCK),
+                in_=sums_psum[block][:, 0 : BLOCK_TENSOR_SUMS * SUMS_PER_BLOCK].rearrange(
+                    "k (x s) -> k s x", s=SUMS_PER_BLOCK
+                ),
+            )
+            partial[block] = partial_tile
+
+        def gather_sums(block):
+            gathered = node_psum.tile([P, BLOCK_TENSOR_SUMS], F32, tag="node")
+            for s in range(SUMS_PER_BLOCK):
+                nc.tensor.matmul(
+                    out=gathered[:],
+                    lhsT=gather[:, s, :],
+                    rhs=partial[block][:, s * BLOCK_TENSOR_SUMS : (s + 1) * BLOCK_TENSOR_SUMS],
+                    start=(s == 0),
+                    stop=(s == SUMS_PER_BLOCK - 1),
+                )
+            sums_tensor[block] = gathered
+
+        def scale_relations(block):
+            for u in range(2):
+                rel_view = sup_rows[block][:, u, :, D_NODE // 2 :].rearrange("i (g r) x -> i g r x", g=N_GROUPS)
+                relf_view = relf_turned[:, u].rearrange("i (g r) x -> i g r x", g=N_GROUPS)
+                nc.vector.tensor_tensor(
+                    out=rel_view[:, :, 0:TENSOR_SUMS, :],
+                    in0=relf_view[:, :, 0:TENSOR_SUMS, :],
+                    in1=sums_tensor[block][:]
+                    .rearrange("i (g r) -> i g r", g=N_GROUPS)
+                    .unsqueeze(3)
+                    .to_broadcast([P, N_GROUPS, TENSOR_SUMS, D_REL // 2]),
+                    op=ALU.mult,
+                )
+                nc.vector.tensor_tensor(
+                    out=rel_view[:, :, TENSOR_SUMS:GROUP, :],
+                    in0=relf_view[:, :, TENSOR_SUMS:GROUP, :],
+                    in1=sums_vector[block][:]
+                    .unsqueeze(3)
+                    .to_broadcast([P, N_GROUPS, VECTOR_SUMS, D_REL // 2]),
+                    op=ALU.mult,
+                )
+
+        def transpose_supports(block):
+            s_words = sup_rows[block][:].rearrange("i u r x -> i (u r x)").bitcast(F32)
+            sup_tile = block_pool.tile([P, SUP_PASSES * P * PACK], BF16, align_bytes=64)
+            sup_words = sup_tile[:].bitcast(F32).rearrange("p (q i u) -> p q i u", q=SUP_PASSES, u=2)
+            for q in range(0, SUP_PASSES, 2):
+                sup_t = turned_psum.tile([P, 2, 2, P], F32, tag="turned")
+                for k in range(2):
+                    for u in range(2):
+                        first = u * (KS // 4) + (q + k) * P
+                        nc.tensor.transpose(
+                            out=sup_t[:, k, u, :], in_=s_words[:, first : first + P], identity=ident_f32[:]
+                        )
+                nc.scalar.copy(
+                    out=sup_words[:, q : q + 2], in_=sup_t[:].rearrange("p k u i -> p k i u")
+                )
+            sup_grouped[block] = sup_tile
+
+        def quantise_supports(block):
+            codes = block_pool.tile([P, SUP_PASSES * P], U32, align_bytes=64)
+            scales = block_pool.tile([P, SUP_PASSES * P], U8, align_bytes=64)
+            for first, width in ((0, 4 * P), (4 * P, 2 * P)):
+                nc.vector.quantize_mx(
+                    out=codes[:, first : first + width].bitcast(FP8X4),
+                    scales=scales[:, first : first + width],
+                    in_=sup_grouped[block][:, PACK * first : PACK * (first + width)],
+                )
+            sup_codes[block] = codes
+            sup_scales[block] = scales
+
+        def project(block):
+            out_psum = single_psum.tile([P, BASES], F32)
+            for q in range(SUP_PASSES):
+                nc.tensor.matmul_mx(
+                    out=out_psum[:],
+                    lhsT=sup_codes[block][:, q * P : (q + 1) * P].bitcast(FP8X4),
+                    lhsT_scale=sup_scales[block][:, q * P : (q + 1) * P],
+                    rhs=w_codes[:, q * BASES : (q + 1) * BASES].bitcast(FP8X4),
+                    rhs_scale=w_scales[:, q * BASES : (q + 1) * BASES],
+                    start=(q == 0),
+                    stop=(q == SUP_PASSES - 1),
+                )
+            out_rows = block_pool.tile([P, BASES], F32)
+            nc.scalar.copy(out=out_rows[:], in_=out_psum[:])
+            nc.scalar.dma_start(out=out[0, block * P : (block + 1) * P, :], in_=out_rows[:])
+
+        for step in range(N_ROUNDS + PROJECT_LAG):
+            if is_round(step):
+                load_round(step)
+                sum_on_vector(step)
+            if step == WEIGHT_STEP:
+                prepare_weights()
+            if is_round(step):
+                transpose_round(step)
+            if block_ending_with(step - TURN_LAG) is not None:
+                transpose_supports(block_ending_with(step - TURN_LAG))
+            if is_round(step - QUANTISE_LAG):
+                sum_on_tensor(step - QUANTISE_LAG)
+                quantise_round(step - QUANTISE_LAG)
+            if block_ending_with(step - COLLECT_LAG) is not None:
+                collect_sums(block_ending_with(step - COLLECT_LAG))
+            if block_ending_with(step - GATHER_LAG) is not None:
+                gather_sums(block_ending_with(step - GATHER_LAG))
+                scale_relations(block_ending_with(step - GATHER_LAG))
+            if block_ending_with(step - SUPPORT_LAG) is not None:
+                quantise_supports(block_ending_with(step - SUPPORT_LAG))
+            if is_round(step - MULTIPLY_LAG):
+                multiply_round(step - MULTIPLY_LAG)
+            if block_ending_with(step - PROJECT_LAG) is not None:
+                project(block_ending_with(step - PROJECT_LAG))

@@ -31,20 +31,18 @@ J_PASSES = NODES // K_PASS
 KS = RELATIONS * D_SUPPORT
 SUP_PASSES = KS // K_PASS
 
-TENSOR_SUMS = 2
-VECTOR_SUMS = GROUP - TENSOR_SUMS
-BLOCK_TENSOR_SUMS = N_GROUPS * TENSOR_SUMS
 ROWS_PER_SUM = P // PACK
 SUMS_PER_BLOCK = P // ROWS_PER_SUM
-SUM_WIDTH = 32
+SUM_WIDTH = 16
 
-QUANTISE_LAG = 1
-MULTIPLY_LAG = 2
-COLLECT_LAG = 1
-GATHER_LAG = 2
-TURN_LAG = 3
-SUPPORT_LAG = 4
-PROJECT_LAG = 5
+TRANSPOSE_LAG = 1
+QUANTISE_LAG = 2
+MULTIPLY_LAG = 3
+COLLECT_LAG = 2
+GATHER_LAG = 3
+TURN_LAG = 4
+SUPPORT_LAG = 5
+PROJECT_LAG = 6
 WEIGHT_STEP = 2
 
 FLOPS = 2 * RELATIONS * NODES * NODES * D_NODE + 2 * NODES * RELATIONS * D_SUPPORT * BASES
@@ -154,10 +152,10 @@ def tile_relationalgraphconvolution_pa_kernel(
                 )
 
         a_rows = {}
+        split = {}
         grouped = {}
         a_codes = {}
         a_scales = {}
-        sums_vector = {}
         sums_psum = {}
         sup_rows = {}
         sup_grouped = {}
@@ -173,26 +171,16 @@ def tile_relationalgraphconvolution_pa_kernel(
             )
             a_rows[n] = a_tile
 
-        def sum_on_vector(n):
-            block, group = divmod(n, N_GROUPS)
-            if group == 0:
-                sums_tile = block_pool.tile([P, N_GROUPS, VECTOR_SUMS], F32)
-                sums_vector[block] = sums_tile
-            for v in range(VECTOR_SUMS):
-                r = TENSOR_SUMS + v
-                scratch = round_pool.tile([P, NODES], BF16)
-                nc.vector.tensor_scalar(
-                    out=scratch[:],
-                    in0=a_rows[n][:, r * NODES : (r + 1) * NODES],
-                    scalar1=1.0,
-                    scalar2=None,
-                    op0=ALU.mult,
-                    op1=ALU.add,
-                    accum_out=sums_vector[block][:, group, v : v + 1],
-                )
+        def split_round(n):
+            split_tile = round_pool.tile([P, GROUP * NODES], BF16)
+            nc.vector.tensor_copy(
+                out=split_tile[:].bitcast(F32).rearrange("i (u w) -> i u w", u=2),
+                in_=a_rows[n][:].bitcast(F32).rearrange("i (w u) -> i u w", u=2),
+            )
+            split[n] = split_tile
 
         def transpose_round(n):
-            a_words = a_rows[n][:].bitcast(F32)
+            a_words = split[n][:].bitcast(F32)
             g_tile = round_pool.tile([P, GROUP * NODES], BF16, align_bytes=64)
             g_words = g_tile[:].bitcast(F32).rearrange(
                 "p (r c i u) -> p r c i u", r=GROUP, c=J_PASSES, u=2
@@ -201,10 +189,10 @@ def tile_relationalgraphconvolution_pa_kernel(
                 a_t = turned_psum.tile([P, PACK, P], F32, tag="turned")
                 for c in range(J_PASSES):
                     for u in range(2):
-                        first = r * (NODES // 2) + c * 2 * P + u
+                        first = u * (GROUP * NODES // 4) + (r * J_PASSES + c) * P
                         nc.tensor.transpose(
                             out=a_t[:, 2 * c + u, :],
-                            in_=a_words[:, first : first + 2 * P - 1 : 2],
+                            in_=a_words[:, first : first + P],
                             identity=ident_f32[:],
                         )
                 nc.scalar.copy(
@@ -216,12 +204,12 @@ def tile_relationalgraphconvolution_pa_kernel(
             block, group = divmod(n, N_GROUPS)
             if group == 0:
                 sums_tile = single_psum.tile(
-                    [P, BLOCK_TENSOR_SUMS * SUMS_PER_BLOCK + SUM_WIDTH - 1], F32
+                    [P, RELATIONS * SUMS_PER_BLOCK + SUM_WIDTH - 1], F32
                 )
                 sums_psum[block] = sums_tile
-            for r in range(TENSOR_SUMS):
+            for r in range(GROUP):
                 for s in range(SUMS_PER_BLOCK):
-                    column = (group * TENSOR_SUMS + r) * SUMS_PER_BLOCK + s
+                    column = (group * GROUP + r) * SUMS_PER_BLOCK + s
                     for c in range(J_PASSES):
                         first = ((r * J_PASSES + c) * P + s * ROWS_PER_SUM) * PACK
                         nc.tensor.matmul(
@@ -266,53 +254,42 @@ def tile_relationalgraphconvolution_pa_kernel(
             )
 
         partial = {}
-        sums_tensor = {}
+        sums = {}
         sup_codes = {}
         sup_scales = {}
 
         def collect_sums(block):
-            partial_tile = block_pool.tile([P, SUMS_PER_BLOCK * BLOCK_TENSOR_SUMS], F32)
+            partial_tile = block_pool.tile([P, SUMS_PER_BLOCK * RELATIONS], F32)
             nc.scalar.copy(
                 out=partial_tile[:].rearrange("k (s x) -> k s x", s=SUMS_PER_BLOCK),
-                in_=sums_psum[block][:, 0 : BLOCK_TENSOR_SUMS * SUMS_PER_BLOCK].rearrange(
+                in_=sums_psum[block][:, 0 : RELATIONS * SUMS_PER_BLOCK].rearrange(
                     "k (x s) -> k s x", s=SUMS_PER_BLOCK
                 ),
             )
             partial[block] = partial_tile
 
         def gather_sums(block):
-            gathered = node_psum.tile([P, BLOCK_TENSOR_SUMS], F32, tag="node")
+            gathered = node_psum.tile([P, RELATIONS], F32, tag="node")
             for s in range(SUMS_PER_BLOCK):
                 nc.tensor.matmul(
                     out=gathered[:],
                     lhsT=gather[:, s, :],
-                    rhs=partial[block][:, s * BLOCK_TENSOR_SUMS : (s + 1) * BLOCK_TENSOR_SUMS],
+                    rhs=partial[block][:, s * RELATIONS : (s + 1) * RELATIONS],
                     start=(s == 0),
                     stop=(s == SUMS_PER_BLOCK - 1),
                 )
-            sums_tensor[block] = gathered
+            sums[block] = gathered
 
         def scale_relations(block):
-            for u in range(2):
-                rel_view = sup_rows[block][:, u, :, D_NODE // 2 :].rearrange("i (g r) x -> i g r x", g=N_GROUPS)
-                relf_view = relf_turned[:, u].rearrange("i (g r) x -> i g r x", g=N_GROUPS)
-                nc.vector.tensor_tensor(
-                    out=rel_view[:, :, 0:TENSOR_SUMS, :],
-                    in0=relf_view[:, :, 0:TENSOR_SUMS, :],
-                    in1=sums_tensor[block][:]
-                    .rearrange("i (g r) -> i g r", g=N_GROUPS)
-                    .unsqueeze(3)
-                    .to_broadcast([P, N_GROUPS, TENSOR_SUMS, D_REL // 2]),
-                    op=ALU.mult,
-                )
-                nc.vector.tensor_tensor(
-                    out=rel_view[:, :, TENSOR_SUMS:GROUP, :],
-                    in0=relf_view[:, :, TENSOR_SUMS:GROUP, :],
-                    in1=sums_vector[block][:]
-                    .unsqueeze(3)
-                    .to_broadcast([P, N_GROUPS, VECTOR_SUMS, D_REL // 2]),
-                    op=ALU.mult,
-                )
+            nc.vector.tensor_tensor(
+                out=sup_rows[block][:, :, :, D_NODE // 2 :],
+                in0=relf_turned[:],
+                in1=sums[block][:]
+                .unsqueeze(1)
+                .unsqueeze(3)
+                .to_broadcast([P, 2, RELATIONS, D_REL // 2]),
+                op=ALU.mult,
+            )
 
         def transpose_supports(block):
             s_words = sup_rows[block][:].rearrange("i u r x -> i (u r x)").bitcast(F32)
@@ -362,11 +339,11 @@ def tile_relationalgraphconvolution_pa_kernel(
         for step in range(N_ROUNDS + PROJECT_LAG):
             if is_round(step):
                 load_round(step)
-                sum_on_vector(step)
+                split_round(step)
             if step == WEIGHT_STEP:
                 prepare_weights()
-            if is_round(step):
-                transpose_round(step)
+            if is_round(step - TRANSPOSE_LAG):
+                transpose_round(step - TRANSPOSE_LAG)
             if block_ending_with(step - TURN_LAG) is not None:
                 transpose_supports(block_ending_with(step - TURN_LAG))
             if is_round(step - QUANTISE_LAG):

@@ -68,7 +68,7 @@ def tile_relationalgraphconvolution_pa_kernel(
         adj_pool = ctx.enter_context(tc.tile_pool(name="adj", bufs=4))
         round_pool = ctx.enter_context(tc.tile_pool(name="round", bufs=3))
         block_pool = ctx.enter_context(tc.tile_pool(name="block", bufs=2))
-        turned_psum = ctx.enter_context(tc.psum_pool(name="turned", bufs=4))
+        turned_psum = ctx.enter_context(tc.psum_pool(name="turned", bufs=5))
         node_psum = ctx.enter_context(tc.psum_pool(name="node", bufs=2))
         single_psum = ctx.enter_context(tc.psum_pool(name="single", bufs=1))
 
@@ -321,7 +321,7 @@ def tile_relationalgraphconvolution_pa_kernel(
             sup_scales[block] = scales
 
         def project(block):
-            out_psum = single_psum.tile([P, BASES], F32)
+            out_psum = node_psum.tile([P, BASES], F32, tag="node")
             for q in range(SUP_PASSES):
                 nc.tensor.matmul_mx(
                     out=out_psum[:],
@@ -339,16 +339,21 @@ def tile_relationalgraphconvolution_pa_kernel(
         for step in range(N_ROUNDS + PROJECT_LAG):
             if is_round(step):
                 load_round(step)
-                split_round(step)
-            if step == WEIGHT_STEP:
-                prepare_weights()
+            if is_round(step - MULTIPLY_LAG):
+                multiply_round(step - MULTIPLY_LAG)
+            if block_ending_with(step - PROJECT_LAG) is not None:
+                project(block_ending_with(step - PROJECT_LAG))
             if is_round(step - TRANSPOSE_LAG):
                 transpose_round(step - TRANSPOSE_LAG)
             if block_ending_with(step - TURN_LAG) is not None:
                 transpose_supports(block_ending_with(step - TURN_LAG))
+            if step == WEIGHT_STEP:
+                prepare_weights()
             if is_round(step - QUANTISE_LAG):
-                sum_on_tensor(step - QUANTISE_LAG)
                 quantise_round(step - QUANTISE_LAG)
+                sum_on_tensor(step - QUANTISE_LAG)
+            if is_round(step):
+                split_round(step)
             if block_ending_with(step - COLLECT_LAG) is not None:
                 collect_sums(block_ending_with(step - COLLECT_LAG))
             if block_ending_with(step - GATHER_LAG) is not None:
@@ -356,7 +361,3 @@ def tile_relationalgraphconvolution_pa_kernel(
                 scale_relations(block_ending_with(step - GATHER_LAG))
             if block_ending_with(step - SUPPORT_LAG) is not None:
                 quantise_supports(block_ending_with(step - SUPPORT_LAG))
-            if is_round(step - MULTIPLY_LAG):
-                multiply_round(step - MULTIPLY_LAG)
-            if block_ending_with(step - PROJECT_LAG) is not None:
-                project(block_ending_with(step - PROJECT_LAG))

@@ -33,23 +33,32 @@ SUP_PASSES = KS // K_PASS
 
 ROWS_PER_SUM = P // PACK
 SUMS_PER_BLOCK = P // ROWS_PER_SUM
-SUM_WIDTH = 16
+SUM_WIDTH = 20
+VECTOR_SUMS = 1
+TENSOR_SUMS = GROUP - VECTOR_SUMS
+BLOCK_TENSOR_SUMS = N_GROUPS * TENSOR_SUMS
 
-TRANSPOSE_LAG = 1
-QUANTISE_LAG = 2
-MULTIPLY_LAG = 3
-COLLECT_LAG = 2
-GATHER_LAG = 3
-TURN_LAG = 4
-SUPPORT_LAG = 5
-PROJECT_LAG = 6
-WEIGHT_STEP = 2
+TRANSPOSE_LAG = 2
+QUANTISE_LAG = 3
+SUM_LAG = 3
+MULTIPLY_LAG = 5
+GATHER_LAG = 4
+RELATION_LAG = 5
+TURN_LAG = 7
+SUPPORT_LAG = 8
+PROJECT_LAG = 10
+WEIGHT_LOAD_STEP = 1
+WEIGHT_TURN_STEP = 2
 
 FLOPS = 2 * RELATIONS * NODES * NODES * D_NODE + 2 * NODES * RELATIONS * D_SUPPORT * BASES
 
 
 def is_round(n):
     return 0 <= n < N_ROUNDS
+
+
+def is_pass(q):
+    return 0 <= q < SUP_PASSES
 
 
 def block_ending_with(n):
@@ -66,8 +75,8 @@ def tile_relationalgraphconvolution_pa_kernel(
         ctx.enter_context(tc.manual_schedule())
         const = ctx.enter_context(tc.tile_pool(name="const", bufs=1))
         adj_pool = ctx.enter_context(tc.tile_pool(name="adj", bufs=4))
-        round_pool = ctx.enter_context(tc.tile_pool(name="round", bufs=3))
-        block_pool = ctx.enter_context(tc.tile_pool(name="block", bufs=2))
+        round_pool = ctx.enter_context(tc.tile_pool(name="round", bufs=4))
+        block_pool = ctx.enter_context(tc.tile_pool(name="block", bufs=3))
         turned_psum = ctx.enter_context(tc.psum_pool(name="turned", bufs=5))
         node_psum = ctx.enter_context(tc.psum_pool(name="node", bufs=2))
         single_psum = ctx.enter_context(tc.psum_pool(name="single", bufs=1))
@@ -114,44 +123,52 @@ def tile_relationalgraphconvolution_pa_kernel(
         w_scales = const.tile([P, SUP_PASSES * BASES], U8, align_bytes=64)
         relf_turned = const.tile([P, 2, RELATIONS, D_REL // 2], BF16)
 
-        def prepare_weights():
-            w_rows = const.tile([P, BASE_HALVES, KS], BF16)
+        w_rows = const.tile([P, BASE_HALVES, KS], BF16)
+        w_grouped = const.tile([P, SUP_PASSES, BASES * PACK], BF16, align_bytes=64)
+        relf_all = const.tile([P, RELATIONS * D_REL], BF16)
+
+        def load_weights():
             nc.sync.dma_start(out=w_rows[:], in_=Wb.rearrange("(h p) k -> p h k", p=P))
-            relf_all = const.tile([P, RELATIONS * D_REL], BF16)
             nc.sync.dma_start(
                 out=relf_all[:],
                 in_=relation_features[0].rearrange("r e -> (r e)").partition_broadcast(P),
             )
+
+        def turn_relation_features():
             nc.vector.tensor_copy(
                 out=relf_turned[:].rearrange("p u r (x e) -> p u (r x) e", e=2),
                 in_=relf_all[:].rearrange("p (rx u e) -> p u rx e", u=2, e=2),
             )
+
+        def transpose_weights(q):
             w_words = w_rows[:].rearrange("p h k -> p (h k)").bitcast(F32)
-            w_grouped = const.tile([P, SUP_PASSES, BASES * PACK], BF16, align_bytes=64)
-            for q in range(SUP_PASSES):
-                w_t = turned_psum.tile([P, BASE_HALVES, 2, P], F32, tag="turned")
-                for h in range(BASE_HALVES):
-                    for u in range(2):
-                        first = h * (KS // 2) + q * 2 * P + u
-                        nc.tensor.transpose(
-                            out=w_t[:, h, u, :],
-                            in_=w_words[:, first : first + 2 * P - 1 : 2],
-                            identity=ident_f32[:],
-                        )
-                copy = nc.vector.tensor_copy if q % 2 == 0 else nc.scalar.copy
-                copy(
-                    out=w_grouped[:, q].bitcast(F32).rearrange("p (h b u) -> p h b u", h=BASE_HALVES, u=2),
-                    in_=w_t[:].rearrange("p h u b -> p h b u"),
-                )
-            w_flat = w_grouped[:].rearrange("p q x -> p (q x)")
-            for first, width in ((0, 4 * BASES), (4 * BASES, 2 * BASES)):
-                nc.vector.quantize_mx(
-                    out=w_codes[:, first : first + width].bitcast(FP8X4),
-                    scales=w_scales[:, first : first + width],
-                    in_=w_flat[:, PACK * first : PACK * (first + width)],
-                )
+            w_t = turned_psum.tile([P, BASE_HALVES, 2, P], F32, tag="turned")
+            for h in range(BASE_HALVES):
+                for u in range(2):
+                    first = h * (KS // 2) + q * 2 * P + u
+                    nc.tensor.transpose(
+                        out=w_t[:, h, u, :],
+                        in_=w_words[:, first : first + 2 * P - 1 : 2],
+                        identity=ident_f32[:],
+                    )
+            nc.scalar.copy(
+                out=w_grouped[:, q].bitcast(F32).rearrange("p (h b u) -> p h b u", h=BASE_HALVES, u=2),
+                in_=w_t[:].rearrange("p h u b -> p h b u"),
+            )
+
+        def quantise_weights(q):
+            nc.vector.quantize_mx(
+                out=w_codes[:, q * BASES : (q + 1) * BASES].bitcast(FP8X4),
+                scales=w_scales[:, q * BASES : (q + 1) * BASES],
+                in_=w_grouped[:, q],
+            )
 
         a_rows = {}
+        turned = {}
+        node_banks = {}
+        sup_banks = {}
+        out_banks = {}
+        gathered_banks = {}
         split = {}
         grouped = {}
         a_codes = {}
@@ -172,19 +189,37 @@ def tile_relationalgraphconvolution_pa_kernel(
             a_rows[n] = a_tile
 
         def split_round(n):
+            block, group = divmod(n, N_GROUPS)
+            if group == 0:
+                sums_tile = block_pool.tile([P, RELATIONS], F32)
+                sums[block] = sums_tile
             split_tile = round_pool.tile([P, GROUP * NODES], BF16)
-            nc.vector.tensor_copy(
-                out=split_tile[:].bitcast(F32).rearrange("i (u w) -> i u w", u=2),
-                in_=a_rows[n][:].bitcast(F32).rearrange("i (w u) -> i u w", u=2),
-            )
             split[n] = split_tile
+            copied = TENSOR_SUMS * NODES // 2
+            nc.vector.tensor_copy(
+                out=split_tile[:].bitcast(F32).rearrange("i (u w) -> i u w", u=2)[:, :, 0 : copied // 2],
+                in_=a_rows[n][:].bitcast(F32)[:, 0:copied].rearrange("i (w u) -> i u w", u=2),
+            )
+
+        def split_and_sum(n):
+            block, group = divmod(n, N_GROUPS)
+            for r in range(TENSOR_SUMS, GROUP):
+                nc.vector.tensor_scalar(
+                    out=split[n][:].rearrange("i (u r w e) -> i r u w e", u=2, r=GROUP, e=2)[:, r],
+                    in0=a_rows[n][:, r * NODES : (r + 1) * NODES].rearrange(
+                        "i (w u e) -> i u w e", u=2, e=2
+                    ),
+                    scalar1=1.0,
+                    scalar2=None,
+                    op0=ALU.mult,
+                    op1=ALU.add,
+                    accum_out=sums[block][:, group * GROUP + r : group * GROUP + r + 1],
+                )
 
         def transpose_round(n):
             a_words = split[n][:].bitcast(F32)
             g_tile = round_pool.tile([P, GROUP * NODES], BF16, align_bytes=64)
-            g_words = g_tile[:].bitcast(F32).rearrange(
-                "p (r c i u) -> p r c i u", r=GROUP, c=J_PASSES, u=2
-            )
+            turned[n] = []
             for r in range(GROUP):
                 a_t = turned_psum.tile([P, PACK, P], F32, tag="turned")
                 for c in range(J_PASSES):
@@ -195,21 +230,28 @@ def tile_relationalgraphconvolution_pa_kernel(
                             in_=a_words[:, first : first + P],
                             identity=ident_f32[:],
                         )
-                nc.scalar.copy(
-                    out=g_words[:, r], in_=a_t[:].rearrange("p (c u) i -> p c i u", u=2)
-                )
+                turned[n].append(a_t)
             grouped[n] = g_tile
+
+        def empty_turned(n):
+            g_words = grouped[n][:].bitcast(F32).rearrange(
+                "p (r c i u) -> p r c i u", r=GROUP, c=J_PASSES, u=2
+            )
+            for r in range(GROUP):
+                nc.scalar.copy(
+                    out=g_words[:, r], in_=turned[n][r][:].rearrange("p (c u) i -> p c i u", u=2)
+                )
 
         def sum_on_tensor(n):
             block, group = divmod(n, N_GROUPS)
             if group == 0:
                 sums_tile = single_psum.tile(
-                    [P, RELATIONS * SUMS_PER_BLOCK + SUM_WIDTH - 1], F32
+                    [P, BLOCK_TENSOR_SUMS * SUMS_PER_BLOCK + SUM_WIDTH - 1], F32
                 )
                 sums_psum[block] = sums_tile
-            for r in range(GROUP):
+            for r in range(TENSOR_SUMS):
                 for s in range(SUMS_PER_BLOCK):
-                    column = (group * GROUP + r) * SUMS_PER_BLOCK + s
+                    column = (group * TENSOR_SUMS + r) * SUMS_PER_BLOCK + s
                     for c in range(J_PASSES):
                         first = ((r * J_PASSES + c) * P + s * ROWS_PER_SUM) * PACK
                         nc.tensor.matmul(
@@ -246,11 +288,15 @@ def tile_relationalgraphconvolution_pa_kernel(
                         start=(c == 0),
                         stop=(c == J_PASSES - 1),
                     )
+            node_banks[n] = node
+
+        def empty_node(n):
+            block, group = divmod(n, N_GROUPS)
             nc.scalar.copy(
                 out=sup_rows[block][:].rearrange("i u r x -> i r u x")[
                     :, group * GROUP : (group + 1) * GROUP, :, 0 : D_NODE // 2
                 ],
-                in_=node[:].rearrange("i r (u x) -> i r u x", u=2),
+                in_=node_banks[n][:].rearrange("i r (u x) -> i r u x", u=2),
             )
 
         partial = {}
@@ -259,26 +305,32 @@ def tile_relationalgraphconvolution_pa_kernel(
         sup_scales = {}
 
         def collect_sums(block):
-            partial_tile = block_pool.tile([P, SUMS_PER_BLOCK * RELATIONS], F32)
+            partial_tile = block_pool.tile([P, SUMS_PER_BLOCK * BLOCK_TENSOR_SUMS], F32)
             nc.scalar.copy(
                 out=partial_tile[:].rearrange("k (s x) -> k s x", s=SUMS_PER_BLOCK),
-                in_=sums_psum[block][:, 0 : RELATIONS * SUMS_PER_BLOCK].rearrange(
+                in_=sums_psum[block][:, 0 : BLOCK_TENSOR_SUMS * SUMS_PER_BLOCK].rearrange(
                     "k (x s) -> k s x", s=SUMS_PER_BLOCK
                 ),
             )
             partial[block] = partial_tile
 
         def gather_sums(block):
-            gathered = node_psum.tile([P, RELATIONS], F32, tag="node")
+            gathered = node_psum.tile([P, BLOCK_TENSOR_SUMS], F32, tag="node")
             for s in range(SUMS_PER_BLOCK):
                 nc.tensor.matmul(
                     out=gathered[:],
                     lhsT=gather[:, s, :],
-                    rhs=partial[block][:, s * RELATIONS : (s + 1) * RELATIONS],
+                    rhs=partial[block][:, s * BLOCK_TENSOR_SUMS : (s + 1) * BLOCK_TENSOR_SUMS],
                     start=(s == 0),
                     stop=(s == SUMS_PER_BLOCK - 1),
                 )
-            sums[block] = gathered
+            gathered_banks[block] = gathered
+
+        def empty_gathered(block):
+            nc.scalar.copy(
+                out=sums[block][:].rearrange("i (g r) -> i g r", r=GROUP)[:, :, 0:TENSOR_SUMS],
+                in_=gathered_banks[block][:].rearrange("i (g r) -> i g r", r=TENSOR_SUMS),
+            )
 
         def scale_relations(block):
             nc.vector.tensor_tensor(
@@ -294,7 +346,7 @@ def tile_relationalgraphconvolution_pa_kernel(
         def transpose_supports(block):
             s_words = sup_rows[block][:].rearrange("i u r x -> i (u r x)").bitcast(F32)
             sup_tile = block_pool.tile([P, SUP_PASSES * P * PACK], BF16, align_bytes=64)
-            sup_words = sup_tile[:].bitcast(F32).rearrange("p (q i u) -> p q i u", q=SUP_PASSES, u=2)
+            sup_banks[block] = []
             for q in range(0, SUP_PASSES, 2):
                 sup_t = turned_psum.tile([P, 2, 2, P], F32, tag="turned")
                 for k in range(2):
@@ -303,10 +355,15 @@ def tile_relationalgraphconvolution_pa_kernel(
                         nc.tensor.transpose(
                             out=sup_t[:, k, u, :], in_=s_words[:, first : first + P], identity=ident_f32[:]
                         )
-                nc.scalar.copy(
-                    out=sup_words[:, q : q + 2], in_=sup_t[:].rearrange("p k u i -> p k i u")
-                )
+                sup_banks[block].append(sup_t)
             sup_grouped[block] = sup_tile
+
+        def empty_supports(block):
+            sup_words = sup_grouped[block][:].bitcast(F32).rearrange("p (q i u) -> p q i u", q=SUP_PASSES, u=2)
+            for q in range(0, SUP_PASSES, 2):
+                nc.scalar.copy(
+                    out=sup_words[:, q : q + 2], in_=sup_banks[block][q // 2][:].rearrange("p k u i -> p k i u")
+                )
 
         def quantise_supports(block):
             codes = block_pool.tile([P, SUP_PASSES * P], U32, align_bytes=64)
@@ -332,32 +389,49 @@ def tile_relationalgraphconvolution_pa_kernel(
                     start=(q == 0),
                     stop=(q == SUP_PASSES - 1),
                 )
+            out_banks[block] = out_psum
+
+        def store(block):
             out_rows = block_pool.tile([P, BASES], F32)
-            nc.scalar.copy(out=out_rows[:], in_=out_psum[:])
+            nc.scalar.copy(out=out_rows[:], in_=out_banks[block][:])
             nc.scalar.dma_start(out=out[0, block * P : (block + 1) * P, :], in_=out_rows[:])
 
         for step in range(N_ROUNDS + PROJECT_LAG):
             if is_round(step):
                 load_round(step)
-            if is_round(step - MULTIPLY_LAG):
-                multiply_round(step - MULTIPLY_LAG)
-            if block_ending_with(step - PROJECT_LAG) is not None:
-                project(block_ending_with(step - PROJECT_LAG))
+            if step == WEIGHT_LOAD_STEP:
+                load_weights()
             if is_round(step - TRANSPOSE_LAG):
                 transpose_round(step - TRANSPOSE_LAG)
+                empty_turned(step - TRANSPOSE_LAG)
             if block_ending_with(step - TURN_LAG) is not None:
                 transpose_supports(block_ending_with(step - TURN_LAG))
-            if step == WEIGHT_STEP:
-                prepare_weights()
-            if is_round(step - QUANTISE_LAG):
-                quantise_round(step - QUANTISE_LAG)
-                sum_on_tensor(step - QUANTISE_LAG)
-            if is_round(step):
-                split_round(step)
-            if block_ending_with(step - COLLECT_LAG) is not None:
-                collect_sums(block_ending_with(step - COLLECT_LAG))
+                empty_supports(block_ending_with(step - TURN_LAG))
+            if is_pass(step - WEIGHT_TURN_STEP):
+                transpose_weights(step - WEIGHT_TURN_STEP)
+            if block_ending_with(step - PROJECT_LAG) is not None:
+                project(block_ending_with(step - PROJECT_LAG))
+                store(block_ending_with(step - PROJECT_LAG))
+            if is_round(step - SUM_LAG):
+                sum_on_tensor(step - SUM_LAG)
+            if block_ending_with(step - SUM_LAG) is not None:
+                collect_sums(block_ending_with(step - SUM_LAG))
             if block_ending_with(step - GATHER_LAG) is not None:
                 gather_sums(block_ending_with(step - GATHER_LAG))
-                scale_relations(block_ending_with(step - GATHER_LAG))
+                empty_gathered(block_ending_with(step - GATHER_LAG))
+            if is_round(step - MULTIPLY_LAG):
+                multiply_round(step - MULTIPLY_LAG)
+                empty_node(step - MULTIPLY_LAG)
+            if is_round(step - QUANTISE_LAG):
+                quantise_round(step - QUANTISE_LAG)
+            if block_ending_with(step - RELATION_LAG) is not None:
+                scale_relations(block_ending_with(step - RELATION_LAG))
             if block_ending_with(step - SUPPORT_LAG) is not None:
                 quantise_supports(block_ending_with(step - SUPPORT_LAG))
+            if step == WEIGHT_TURN_STEP:
+                turn_relation_features()
+            if is_pass(step - WEIGHT_TURN_STEP - 1):
+                quantise_weights(step - WEIGHT_TURN_STEP - 1)
+            if is_round(step):
+                split_round(step)
+                split_and_sum(step)

from contextlib import ExitStack

import concourse.masks as masks
import concourse.mybir as mybir

F32 = mybir.dt.float32
BF16 = mybir.dt.bfloat16
U32 = mybir.dt.uint32
U8 = mybir.dt.uint8
FP8X4 = mybir.dt.float8_e4m3fn_x4
ALU = mybir.AluOpType
AXIS = mybir.AxisListType

P = 128
PACK = 4
K_PASS = P * PACK

NODES = 1024
RELATIONS = 16
D_NODE = 128
D_REL = 64
D_SUPPORT = D_NODE + D_REL
BASES = 256
BASE_HALVES = BASES // P

GROUP = 4
N_GROUPS = RELATIONS // GROUP
N_BLOCKS = NODES // P
N_ROUNDS = N_BLOCKS * N_GROUPS
J_PASSES = NODES // K_PASS
KS = RELATIONS * D_SUPPORT
SUP_PASSES = KS // K_PASS

ROWS_PER_SUM = P // PACK
SUMS_PER_BLOCK = P // ROWS_PER_SUM
SUM_WIDTH = 20
VECTOR_SUMS = 1
TENSOR_SUMS = GROUP - VECTOR_SUMS
BLOCK_TENSOR_SUMS = N_GROUPS * TENSOR_SUMS

TRANSPOSE_LAG = 2
QUANTISE_LAG = 3
SUM_LAG = 3
MULTIPLY_LAG = 5
GATHER_LAG = 4
RELATION_LAG = 5
TURN_LAG = 7
SUPPORT_LAG = 8
PROJECT_LAG = 10
WEIGHT_LOAD_STEP = 1
WEIGHT_TURN_STEP = 2

FLOPS = 2 * RELATIONS * NODES * NODES * D_NODE + 2 * NODES * RELATIONS * D_SUPPORT * BASES


def is_round(n):
    return 0 <= n < N_ROUNDS


def is_pass(q):
    return 0 <= q < SUP_PASSES


def block_ending_with(n):
    if is_round(n) and n % N_GROUPS == N_GROUPS - 1:
        return n // N_GROUPS
    return None


def tile_relationalgraphconvolution_pa_kernel(
    tc, node_features, relation_features, adj, Wb, out
):
    nc = tc.nc
    with ExitStack() as ctx:
        ctx.enter_context(tc.manual_schedule())
        const = ctx.enter_context(tc.tile_pool(name="const", bufs=1))
        adj_pool = ctx.enter_context(tc.tile_pool(name="adj", bufs=4))
        round_pool = ctx.enter_context(tc.tile_pool(name="round", bufs=4))
        block_pool = ctx.enter_context(tc.tile_pool(name="block", bufs=3))
        turned_psum = ctx.enter_context(tc.psum_pool(name="turned", bufs=5))
        node_psum = ctx.enter_context(tc.psum_pool(name="node", bufs=2))
        single_psum = ctx.enter_context(tc.psum_pool(name="single", bufs=1))

        ident_f32 = const.tile([P, P], F32)
        masks.make_identity(nc, ident_f32[:])
        ones = const.tile([P, SUM_WIDTH], BF16)
        nc.vector.memset(ones[:], 1.0)
        gather = const.tile([P, SUMS_PER_BLOCK, P], F32)
        nc.vector.memset(gather[:], 0.0)
        for s in range(SUMS_PER_BLOCK):
            nc.vector.tensor_reduce(
                out=gather[:, s, s * ROWS_PER_SUM : (s + 1) * ROWS_PER_SUM],
                in_=ident_f32[:].rearrange("k (x t) -> k x t", t=PACK),
                axis=AXIS.X,
                op=ALU.add,
            )

        nf_rows = const.tile([P, J_PASSES, PACK * D_NODE], BF16)
        nc.sync.dma_start(
            out=nf_rows[:],
            in_=node_features[0].rearrange("(c p t) d -> p c (t d)", p=P, t=PACK),
        )
        nf_grouped = const.tile([P, J_PASSES, D_NODE, PACK], BF16, align_bytes=64)
        for c in range(J_PASSES):
            for u in range(2):
                nc.vector.tensor_copy(
                    out=nf_grouped[:, c, u * D_NODE // 2 : (u + 1) * D_NODE // 2, :].rearrange(
                        "p (x e) t -> p x e t", e=2
                    ),
                    in_=nf_rows[:, c, :].rearrange("p (t x u e) -> p u x e t", t=PACK, u=2, e=2)[
                        :, u
                    ],
                )
        nf_codes = const.tile([P, J_PASSES * D_NODE], U32, align_bytes=64)
        nf_scales = const.tile([P, J_PASSES * D_NODE], U8, align_bytes=64)
        nc.vector.quantize_mx(
            out=nf_codes[:].bitcast(FP8X4),
            scales=nf_scales[:],
            in_=nf_grouped[:].rearrange("p c d t -> p (c d t)"),
        )

        w_codes = const.tile([P, SUP_PASSES * BASES], U32, align_bytes=64)
        w_scales = const.tile([P, SUP_PASSES * BASES], U8, align_bytes=64)
        relf_turned = const.tile([P, 2, RELATIONS, D_REL // 2], BF16)

        w_rows = const.tile([P, BASE_HALVES, KS], BF16)
        w_grouped = const.tile([P, SUP_PASSES, BASES * PACK], BF16, align_bytes=64)
        relf_all = const.tile([P, RELATIONS * D_REL], BF16)

        def load_weights():
            nc.sync.dma_start(out=w_rows[:], in_=Wb.rearrange("(h p) k -> p h k", p=P))
            nc.sync.dma_start(
                out=relf_all[:],
                in_=relation_features[0].rearrange("r e -> (r e)").partition_broadcast(P),
            )

        def turn_relation_features():
            nc.vector.tensor_copy(
                out=relf_turned[:].rearrange("p u r (x e) -> p u (r x) e", e=2),
                in_=relf_all[:].rearrange("p (rx u e) -> p u rx e", u=2, e=2),
            )

        def transpose_weights(q):
            w_words = w_rows[:].rearrange("p h k -> p (h k)").bitcast(F32)
            w_t = turned_psum.tile([P, BASE_HALVES, 2, P], F32, tag="turned")
            for h in range(BASE_HALVES):
                for u in range(2):
                    first = h * (KS // 2) + q * 2 * P + u
                    nc.tensor.transpose(
                        out=w_t[:, h, u, :],
                        in_=w_words[:, first : first + 2 * P - 1 : 2],
                        identity=ident_f32[:],
                    )
            nc.scalar.copy(
                out=w_grouped[:, q].bitcast(F32).rearrange("p (h b u) -> p h b u", h=BASE_HALVES, u=2),
                in_=w_t[:].rearrange("p h u b -> p h b u"),
            )

        def quantise_weights(q):
            nc.vector.quantize_mx(
                out=w_codes[:, q * BASES : (q + 1) * BASES].bitcast(FP8X4),
                scales=w_scales[:, q * BASES : (q + 1) * BASES],
                in_=w_grouped[:, q],
            )

        a_rows = {}
        turned = {}
        node_banks = {}
        sup_banks = {}
        out_banks = {}
        gathered_banks = {}
        split = {}
        grouped = {}
        a_codes = {}
        a_scales = {}
        sums_psum = {}
        sup_rows = {}
        sup_grouped = {}

        def load_round(n):
            block, group = divmod(n, N_GROUPS)
            a_tile = adj_pool.tile([P, GROUP * NODES], BF16)
            nc.sync.dma_start(
                out=a_tile[:].rearrange("i (r j) -> i r j", r=GROUP),
                in_=adj[
                    0, group * GROUP : (group + 1) * GROUP, block * P : (block + 1) * P, :
                ].rearrange("r i j -> i r j"),
            )
            a_rows[n] = a_tile

        def split_round(n):
            block, group = divmod(n, N_GROUPS)
            if group == 0:
                sums_tile = block_pool.tile([P, RELATIONS], F32)
                sums[block] = sums_tile
            split_tile = round_pool.tile([P, GROUP * NODES], BF16)
            split[n] = split_tile
            copied = TENSOR_SUMS * NODES // 2
            nc.vector.tensor_copy(
                out=split_tile[:].bitcast(F32).rearrange("i (u w) -> i u w", u=2)[:, :, 0 : copied // 2],
                in_=a_rows[n][:].bitcast(F32)[:, 0:copied].rearrange("i (w u) -> i u w", u=2),
            )

        def split_and_sum(n):
            block, group = divmod(n, N_GROUPS)
            for r in range(TENSOR_SUMS, GROUP):
                nc.vector.tensor_scalar(
                    out=split[n][:].rearrange("i (u r w e) -> i r u w e", u=2, r=GROUP, e=2)[:, r],
                    in0=a_rows[n][:, r * NODES : (r + 1) * NODES].rearrange(
                        "i (w u e) -> i u w e", u=2, e=2
                    ),
                    scalar1=1.0,
                    scalar2=None,
                    op0=ALU.mult,
                    op1=ALU.add,
                    accum_out=sums[block][:, group * GROUP + r : group * GROUP + r + 1],
                )

        def transpose_round(n):
            a_words = split[n][:].bitcast(F32)
            g_tile = round_pool.tile([P, GROUP * NODES], BF16, align_bytes=64)
            turned[n] = []
            for r in range(GROUP):
                a_t = turned_psum.tile([P, PACK, P], F32, tag="turned")
                for c in range(J_PASSES):
                    for u in range(2):
                        first = u * (GROUP * NODES // 4) + (r * J_PASSES + c) * P
                        nc.tensor.transpose(
                            out=a_t[:, 2 * c + u, :],
                            in_=a_words[:, first : first + P],
                            identity=ident_f32[:],
                        )
                turned[n].append(a_t)
            grouped[n] = g_tile

        def empty_turned(n):
            g_words = grouped[n][:].bitcast(F32).rearrange(
                "p (r c i u) -> p r c i u", r=GROUP, c=J_PASSES, u=2
            )
            for r in range(GROUP):
                nc.scalar.copy(
                    out=g_words[:, r], in_=turned[n][r][:].rearrange("p (c u) i -> p c i u", u=2)
                )

        def sum_on_tensor(n):
            block, group = divmod(n, N_GROUPS)
            if group == 0:
                sums_tile = single_psum.tile(
                    [P, BLOCK_TENSOR_SUMS * SUMS_PER_BLOCK + SUM_WIDTH - 1], F32
                )
                sums_psum[block] = sums_tile
            for r in range(TENSOR_SUMS):
                for s in range(SUMS_PER_BLOCK):
                    column = (group * TENSOR_SUMS + r) * SUMS_PER_BLOCK + s
                    for c in range(J_PASSES):
                        first = ((r * J_PASSES + c) * P + s * ROWS_PER_SUM) * PACK
                        nc.tensor.matmul(
                            out=sums_psum[block][:, column : column + SUM_WIDTH],
                            lhsT=grouped[n][:, first : first + P],
                            rhs=ones[:],
                            start=(c == 0),
                            stop=(c == J_PASSES - 1),
                        )

        def quantise_round(n):
            codes = round_pool.tile([P, GROUP * J_PASSES * P], U32, align_bytes=64)
            scales = round_pool.tile([P, GROUP * J_PASSES * P], U8, align_bytes=64)
            nc.vector.quantize_mx(out=codes[:].bitcast(FP8X4), scales=scales[:], in_=grouped[n][:])
            a_codes[n] = codes
            a_scales[n] = scales

        def multiply_round(n):
            block, group = divmod(n, N_GROUPS)
            if group == 0:
                rows_tile = block_pool.tile([P, 2, RELATIONS, D_SUPPORT // 2], BF16)
                sup_rows[block] = rows_tile
            node = node_psum.tile([P, GROUP, D_NODE], F32, tag="node")
            for r in range(GROUP):
                for c in range(J_PASSES):
                    a_cols = slice((r * J_PASSES + c) * P, (r * J_PASSES + c + 1) * P)
                    nf_cols = slice(c * D_NODE, (c + 1) * D_NODE)
                    nc.tensor.matmul_mx(
                        out=node[:, r, :],
                        lhsT=a_codes[n][:, a_cols].bitcast(FP8X4),
                        lhsT_scale=a_scales[n][:, a_cols],
                        rhs=nf_codes[:, nf_cols].bitcast(FP8X4),
                        rhs_scale=nf_scales[:, nf_cols],
                        start=(c == 0),
                        stop=(c == J_PASSES - 1),
                    )
            node_banks[n] = node

        def empty_node(n):
            block, group = divmod(n, N_GROUPS)
            nc.scalar.copy(
                out=sup_rows[block][:].rearrange("i u r x -> i r u x")[
                    :, group * GROUP : (group + 1) * GROUP, :, 0 : D_NODE // 2
                ],
                in_=node_banks[n][:].rearrange("i r (u x) -> i r u x", u=2),
            )

        partial = {}
        sums = {}
        sup_codes = {}
        sup_scales = {}

        def collect_sums(block):
            partial_tile = block_pool.tile([P, SUMS_PER_BLOCK * BLOCK_TENSOR_SUMS], F32)
            nc.scalar.copy(
                out=partial_tile[:].rearrange("k (s x) -> k s x", s=SUMS_PER_BLOCK),
                in_=sums_psum[block][:, 0 : BLOCK_TENSOR_SUMS * SUMS_PER_BLOCK].rearrange(
                    "k (x s) -> k s x", s=SUMS_PER_BLOCK
                ),
            )
            partial[block] = partial_tile

        def gather_sums(block):
            gathered = node_psum.tile([P, BLOCK_TENSOR_SUMS], F32, tag="node")
            for s in range(SUMS_PER_BLOCK):
                nc.tensor.matmul(
                    out=gathered[:],
                    lhsT=gather[:, s, :],
                    rhs=partial[block][:, s * BLOCK_TENSOR_SUMS : (s + 1) * BLOCK_TENSOR_SUMS],
                    start=(s == 0),
                    stop=(s == SUMS_PER_BLOCK - 1),
                )
            gathered_banks[block] = gathered

        def empty_gathered(block):
            nc.scalar.copy(
                out=sums[block][:].rearrange("i (g r) -> i g r", r=GROUP)[:, :, 0:TENSOR_SUMS],
                in_=gathered_banks[block][:].rearrange("i (g r) -> i g r", r=TENSOR_SUMS),
            )

        def scale_relations(block):
            nc.vector.tensor_tensor(
                out=sup_rows[block][:, :, :, D_NODE // 2 :],
                in0=relf_turned[:],
                in1=sums[block][:]
                .unsqueeze(1)
                .unsqueeze(3)
                .to_broadcast([P, 2, RELATIONS, D_REL // 2]),
                op=ALU.mult,
            )

        def transpose_supports(block):
            s_words = sup_rows[block][:].rearrange("i u r x -> i (u r x)").bitcast(F32)
            sup_tile = block_pool.tile([P, SUP_PASSES * P * PACK], BF16, align_bytes=64)
            sup_banks[block] = []
            for q in range(0, SUP_PASSES, 2):
                sup_t = turned_psum.tile([P, 2, 2, P], F32, tag="turned")
                for k in range(2):
                    for u in range(2):
                        first = u * (KS // 4) + (q + k) * P
                        nc.tensor.transpose(
                            out=sup_t[:, k, u, :], in_=s_words[:, first : first + P], identity=ident_f32[:]
                        )
                sup_banks[block].append(sup_t)
            sup_grouped[block] = sup_tile

        def empty_supports(block):
            sup_words = sup_grouped[block][:].bitcast(F32).rearrange("p (q i u) -> p q i u", q=SUP_PASSES, u=2)
            for q in range(0, SUP_PASSES, 2):
                nc.scalar.copy(
                    out=sup_words[:, q : q + 2], in_=sup_banks[block][q // 2][:].rearrange("p k u i -> p k i u")
                )

        def quantise_supports(block):
            codes = block_pool.tile([P, SUP_PASSES * P], U32, align_bytes=64)
            scales = block_pool.tile([P, SUP_PASSES * P], U8, align_bytes=64)
            for first, width in ((0, 4 * P), (4 * P, 2 * P)):
                nc.vector.quantize_mx(
                    out=codes[:, first : first + width].bitcast(FP8X4),
                    scales=scales[:, first : first + width],
                    in_=sup_grouped[block][:, PACK * first : PACK * (first + width)],
                )
            sup_codes[block] = codes
            sup_scales[block] = scales

        def project(block):
            out_psum = node_psum.tile([P, BASES], F32, tag="node")
            for q in range(SUP_PASSES):
                nc.tensor.matmul_mx(
                    out=out_psum[:],
                    lhsT=sup_codes[block][:, q * P : (q + 1) * P].bitcast(FP8X4),
                    lhsT_scale=sup_scales[block][:, q * P : (q + 1) * P],
                    rhs=w_codes[:, q * BASES : (q + 1) * BASES].bitcast(FP8X4),
                    rhs_scale=w_scales[:, q * BASES : (q + 1) * BASES],
                    start=(q == 0),
                    stop=(q == SUP_PASSES - 1),
                )
            out_banks[block] = out_psum

        def store(block):
            out_rows = block_pool.tile([P, BASES], F32)
            nc.scalar.copy(out=out_rows[:], in_=out_banks[block][:])
            nc.scalar.dma_start(out=out[0, block * P : (block + 1) * P, :], in_=out_rows[:])

        for step in range(N_ROUNDS + PROJECT_LAG):
            if is_round(step):
                load_round(step)
            if step == WEIGHT_LOAD_STEP:
                load_weights()
            if is_round(step - TRANSPOSE_LAG):
                transpose_round(step - TRANSPOSE_LAG)
                empty_turned(step - TRANSPOSE_LAG)
            if block_ending_with(step - TURN_LAG) is not None:
                transpose_supports(block_ending_with(step - TURN_LAG))
                empty_supports(block_ending_with(step - TURN_LAG))
            if is_pass(step - WEIGHT_TURN_STEP):
                transpose_weights(step - WEIGHT_TURN_STEP)
            if block_ending_with(step - PROJECT_LAG) is not None:
                project(block_ending_with(step - PROJECT_LAG))
                store(block_ending_with(step - PROJECT_LAG))
            if is_round(step - SUM_LAG):
                sum_on_tensor(step - SUM_LAG)
            if block_ending_with(step - SUM_LAG) is not None:
                collect_sums(block_ending_with(step - SUM_LAG))
            if block_ending_with(step - GATHER_LAG) is not None:
                gather_sums(block_ending_with(step - GATHER_LAG))
                empty_gathered(block_ending_with(step - GATHER_LAG))
            if is_round(step - MULTIPLY_LAG):
                multiply_round(step - MULTIPLY_LAG)
                empty_node(step - MULTIPLY_LAG)
            if is_round(step - QUANTISE_LAG):
                quantise_round(step - QUANTISE_LAG)
            if block_ending_with(step - RELATION_LAG) is not None:
                scale_relations(block_ending_with(step - RELATION_LAG))
            if block_ending_with(step - SUPPORT_LAG) is not None:
                quantise_supports(block_ending_with(step - SUPPORT_LAG))
            if step == WEIGHT_TURN_STEP:
                turn_relation_features()
            if is_pass(step - WEIGHT_TURN_STEP - 1):
                quantise_weights(step - WEIGHT_TURN_STEP - 1)
            if is_round(step):
                split_round(step)
                split_and_sum(step)
